import numpy as np
import ml_dtypes


def mxq(x, axis, fmt="e4m3"):
    dtype, down = {"e4m3": (ml_dtypes.float8_e4m3fn, 7), "e5m2": (ml_dtypes.float8_e5m2, 14)}[fmt]
    v = np.moveaxis(np.asarray(x, np.float32).astype(ml_dtypes.bfloat16).astype(np.float64), axis, -1)
    blocks = v.reshape(v.shape[:-1] + (-1, 32))
    amax = np.abs(blocks).max(-1, keepdims=True)
    byte = np.maximum(np.where(amax > 0, np.frexp(amax)[1] - 1 + 127, 0) - down, 1)
    scale = np.exp2(byte - 127.0)
    codes = (blocks / scale).astype(np.float32).astype(dtype).astype(np.float64)
    return np.moveaxis((codes * scale).reshape(v.shape), -1, axis)


WIDE = False


def mx_kscale(k):
    if not WIDE:
        return np.ones(k)
    levels = np.array([10, -10, 5, -5, 0])
    if k % 512:
        return np.exp2(np.random.permutation(np.resize(levels, k // 32))).repeat(32)
    a = np.empty((k // 512, 16))
    for p in range(k // 512):
        a[p, :8] = np.random.permutation(np.resize(levels, 8))
        for g in range(8):
            far = levels[np.abs(levels - a[p, g]) >= 10]
            a[p, g + 8] = far[np.random.randint(len(far))]
    return np.exp2(a.ravel()).repeat(32)


BF16 = ml_dtypes.bfloat16


def bf(x):
    return np.asarray(x, np.float32).astype(BF16)


def f64(x):
    return np.asarray(x).astype(np.float64)


M, K, N = 8192, 512, 512


def setup_inputs():
    s = mx_kscale(K)
    return {"A": bf(np.random.standard_normal((M, K)) * s),
            "B": bf(np.random.standard_normal((K, N)) * 2.0 / np.sqrt(K) / s[:, None])}


def reference(A, B):
    C = mxq(np.tril(f64(A)), 1, "e4m3") @ mxq(np.tril(f64(B)), 0, "e4m3")
    return np.tril(C)

@@ -1,0 +1,185 @@
+from contextlib import ExitStack
+
+import concourse.mybir as mybir
+from concourse.masks import make_identity
+
+M, K, N = 8192, 512, 512
+FLOPS = 2 * M * K * N
+
+BF16 = mybir.dt.bfloat16
+F32 = mybir.dt.float32
+U32 = mybir.dt.uint32
+U8 = mybir.dt.uint8
+FP8X4 = mybir.dt.float8_e4m3fn_x4
+MULT = mybir.AluOpType.mult
+IS_LE = mybir.AluOpType.is_le
+
+P = 128
+GROUP = 4
+STORES = ((4,), (8,), (8, 8), (8, 8, 8, 8), (4,))
+CHUNKS = ((512, 4), (1024, 8), (2048, 16), (4096, 32), (0, 4))
+PINNED = True
+VECTOR_EVERY = 8
+HEAD_ON_SCALAR = 2
+MASK_SLOT = 10
+
+
+def tile_modelnew_t_kernel(tc, A, B, out):
+    nc = tc.nc
+    with ExitStack() as ctx:
+        if PINNED:
+            ctx.enter_context(tc.manual_schedule())
+        const = ctx.enter_context(tc.tile_pool(name="const", bufs=1))
+        a_pool = ctx.enter_context(tc.tile_pool(name="a", bufs=1))
+        o_pool = ctx.enter_context(tc.tile_pool(name="o", bufs=1))
+        work = ctx.enter_context(tc.tile_pool(name="work", bufs=3))
+        xt_pool = ctx.enter_context(tc.psum_pool(name="xt", bufs=4))
+        acc_pool = ctx.enter_context(tc.psum_pool(name="acc", bufs=4))
+
+        a_tiles = []
+        b_raw = const.tile([P, 4, N], BF16)
+        nc.sync.dma_start(out=b_raw[:], in_=B.rearrange("(p t) c -> p t c", t=4))
+        for ci, (row0, tiles) in enumerate(CHUNKS):
+            a_sb = a_pool.tile([P, tiles * K], BF16, name="a%d" % ci)
+            nc.sync.dma_start(
+                out=a_sb[:],
+                in_=A[row0 : row0 + P * tiles, :].rearrange("(p t) k -> p (t k)", t=tiles),
+            )
+            a_tiles.append(a_sb)
+
+        ident = const.tile([P, P], F32)
+        make_identity(nc, ident[:])
+        b_diff = const.tile([P, N, 4], F32)
+        nc.gpsimd.iota(
+            b_diff[:], pattern=[[1, N], [-1, 4]], base=0, channel_multiplier=-4,
+            allow_small_or_imprecise_dtypes=True,
+        )
+        a_diff = const.tile([P, K], F32)
+        nc.gpsimd.iota(
+            a_diff[:], pattern=[[1, K]], base=0, channel_multiplier=-4,
+            allow_small_or_imprecise_dtypes=True,
+        )
+
+        b_grp = const.tile([P, N * 4], BF16, align_bytes=64)
+        b_codes = const.tile([P, N], U32, align_bytes=64)
+        b_scl = const.tile([P, N], U8, align_bytes=64)
+
+        def prepare_b():
+            nc.vector.scalar_tensor_tensor(
+                out=b_grp[:].rearrange("p (c t) -> p c t", t=4), in0=b_diff[:], scalar=0.0,
+                in1=b_raw[:].rearrange("p t c -> p c t"), op0=IS_LE, op1=MULT,
+            )
+            nc.vector.quantize_mx(out=b_codes[:].bitcast(FP8X4), scales=b_scl[:], in_=b_grp[:])
+
+        groups = []
+        for ci, (row0, tiles) in enumerate(CHUNKS):
+            for t0 in range(0, tiles, GROUP):
+                groups.append((ci, t0))
+        n_groups = len(groups)
+        masked_group = [g for g in range(n_groups) if CHUNKS[groups[g][0]][0] == 0][0]
+        a_masked = const.tile([P, 4 * K], BF16)
+
+        state = {}
+        counter = [0]
+
+        def mask_a(t):
+            ci = groups[masked_group][0]
+            nc.vector.scalar_tensor_tensor(
+                out=a_masked[:, t * K : (t + 1) * K], in0=a_diff[:], scalar=float(t),
+                in1=a_tiles[ci][:, t * K : (t + 1) * K], op0=IS_LE, op1=MULT,
+            )
+
+        def transposes(g):
+            ci, t0 = groups[g]
+            src = a_masked if g == masked_group else a_tiles[ci]
+            words = src[:].bitcast(F32)
+            banks = []
+            for b in range(GROUP // 2):
+                xt = xt_pool.tile([P, 2, 2, P], F32, name="xt")
+                for r in range(2):
+                    for u in range(2):
+                        col = (t0 + 2 * b + r) * (K // 2)
+                        nc.tensor.transpose(
+                            xt[:, r, u, :], words[:, col + u : col + K // 2 : 2], ident[:]
+                        )
+                banks.append(xt)
+            state[("xt", g)] = banks
+
+        def regroup(g):
+            grp = work.tile([P, GROUP * P * 4], BF16, name="grp", align_bytes=64)
+            view = grp[:].bitcast(F32).rearrange("p (r m u) -> p r m u", r=GROUP, u=2)
+            for b, xt in enumerate(state[("xt", g)]):
+                dst = view[:, 2 * b : 2 * b + 2, :, :]
+                if g < HEAD_ON_SCALAR:
+                    nc.scalar.copy(out=dst, in_=xt[:].rearrange("p r u m -> p r m u"))
+                else:
+                    nc.vector.tensor_copy(out=dst, in_=xt[:].rearrange("p r u m -> p r m u"))
+            state[("grp", g)] = grp
+
+        def quantise(g):
+            grp = state[("grp", g)]
+            codes = work.tile([P, GROUP * P], U32, name="codes", align_bytes=64)
+            scl = work.tile([P, GROUP * P], U8, name="scl", align_bytes=64)
+            nc.vector.quantize_mx(out=codes[:].bitcast(FP8X4), scales=scl[:], in_=grp[:])
+            state[("q", g)] = (codes, scl)
+
+        def multiply(g):
+            codes, scl = state[("q", g)]
+            accs = []
+            for r in range(GROUP):
+                acc = acc_pool.tile([P, N], F32, name="acc")
+                nc.tensor.matmul_mx(
+                    out=acc[:],
+                    lhsT=codes[:, r * P : (r + 1) * P].bitcast(FP8X4),
+                    lhsT_scale=scl[:, r * P : (r + 1) * P],
+                    rhs=b_codes[:].bitcast(FP8X4),
+                    rhs_scale=b_scl[:],
+                    start=True,
+                    stop=True,
+                )
+                accs.append(acc)
+            state[("acc", g)] = accs
+
+        def drain(g):
+            ci, t0 = groups[g]
+            row0, tiles = CHUNKS[ci]
+            first = 0
+            unit = STORES[ci][0]
+            for width in STORES[ci]:
+                if first + width <= t0:
+                    first += width
+                else:
+                    unit = width
+                    break
+            if t0 == first:
+                state["o"] = o_pool.tile([P, unit, N], F32, name="o%d_%d" % (ci, first))
+            o_sb = state["o"]
+            for r, acc in enumerate(state[("acc", g)]):
+                dst = o_sb[:, t0 + r - first, :]
+                counter[0] += 1
+                if counter[0] % VECTOR_EVERY == 0:
+                    nc.vector.tensor_copy(out=dst, in_=acc[:])
+                else:
+                    nc.scalar.copy(out=dst, in_=acc[:])
+            if t0 + GROUP == first + unit:
+                nc.sync.dma_start(
+                    out=out[row0 : row0 + P * tiles, :].rearrange("(p t) n -> p t n", t=tiles)[
+                        :, first : first + unit, :
+                    ],
+                    in_=o_sb[:],
+                )
+
+        prepare_b()
+        for s in range(n_groups + 2):
+            if s < n_groups:
+                transposes(s)
+            if 1 <= s <= n_groups:
+                quantise(s - 1)
+            if s >= 2:
+                multiply(s - 2)
+            if s < n_groups:
+                regroup(s)
+            if MASK_SLOT <= s < MASK_SLOT + 4:
+                mask_a(s - MASK_SLOT)
+            if s >= 2:
+                drain(s - 2)

@@ -47,27 +47,30 @@ def tile_modelnew_t_kernel(tc, A, B, out):
             )
             a_tiles.append(a_sb)
 
-        ident = const.tile([P, P], F32)
-        make_identity(nc, ident[:])
-        b_diff = const.tile([P, N, 4], F32)
-        nc.gpsimd.iota(
-            b_diff[:], pattern=[[1, N], [-1, 4]], base=0, channel_multiplier=-4,
-            allow_small_or_imprecise_dtypes=True,
-        )
         a_diff = const.tile([P, K], F32)
         nc.gpsimd.iota(
             a_diff[:], pattern=[[1, K]], base=0, channel_multiplier=-4,
             allow_small_or_imprecise_dtypes=True,
         )
 
+        ident = const.tile([P, P], F32)
+        make_identity(nc, ident[:])
+        b_keep = const.tile([P, 4, N], BF16)
+        for t in range(4):
+            nc.vector.tensor_scalar(
+                out=b_keep[:, t, :], in0=a_diff[:], scalar1=float(t), scalar2=None, op0=IS_LE
+            )
+
         b_grp = const.tile([P, N * 4], BF16, align_bytes=64)
         b_codes = const.tile([P, N], U32, align_bytes=64)
         b_scl = const.tile([P, N], U8, align_bytes=64)
 
         def prepare_b():
-            nc.vector.scalar_tensor_tensor(
-                out=b_grp[:].rearrange("p (c t) -> p c t", t=4), in0=b_diff[:], scalar=0.0,
-                in1=b_raw[:].rearrange("p t c -> p c t"), op0=IS_LE, op1=MULT,
+            nc.vector.tensor_tensor(
+                out=b_grp[:].rearrange("p (c t) -> p c t", t=4),
+                in0=b_keep[:].rearrange("p t c -> p c t"),
+                in1=b_raw[:].rearrange("p t c -> p c t"),
+                op=MULT,
             )
             nc.vector.quantize_mx(out=b_codes[:].bitcast(FP8X4), scales=b_scl[:], in_=b_grp[:])
 

@@ -16,8 +16,9 @@ IS_LE = mybir.AluOpType.is_le
 
 P = 128
 GROUP = 4
-STORES = ((4,), (8,), (8, 8), (8, 8, 8, 8), (4,))
-CHUNKS = ((512, 4), (1024, 8), (2048, 16), (4096, 32), (0, 4))
+STORES = ((4, 8, 8, 8, 8, 8, 8, 8), (4,))
+LOADS = ((4, 8, 16, 32), (4,))
+CHUNKS = ((512, 60), (0, 4))
 PINNED = True
 VECTOR_EVERY = 8
 HEAD_ON_SCALAR = 2
@@ -41,10 +42,12 @@ def tile_modelnew_t_kernel(tc, A, B, out):
         nc.sync.dma_start(out=b_raw[:], in_=B.rearrange("(p t) c -> p t c", t=4))
         for ci, (row0, tiles) in enumerate(CHUNKS):
             a_sb = a_pool.tile([P, tiles * K], BF16, name="a%d" % ci)
-            nc.sync.dma_start(
-                out=a_sb[:],
-                in_=A[row0 : row0 + P * tiles, :].rearrange("(p t) k -> p (t k)", t=tiles),
-            )
+            rows = A[row0 : row0 + P * tiles, :].rearrange("(p t) k -> p (t k)", t=tiles)
+            t0 = 0
+            for width in LOADS[ci]:
+                part = slice(t0 * K, (t0 + width) * K)
+                nc.sync.dma_start(out=a_sb[:, part], in_=rows[:, part])
+                t0 += width
             a_tiles.append(a_sb)
 
         a_diff = const.tile([P, K], F32)

@@ -13,16 +13,16 @@ U8 = mybir.dt.uint8
 FP8X4 = mybir.dt.float8_e4m3fn_x4
 MULT = mybir.AluOpType.mult
 IS_LE = mybir.AluOpType.is_le
+IS_GE = mybir.AluOpType.is_ge
 
 P = 128
 GROUP = 4
-STORES = ((4, 8, 8, 8, 8, 8, 8, 8), (4,))
-LOADS = ((4, 8, 16, 32), (4,))
-CHUNKS = ((512, 60), (0, 4))
+STORES = ((8, 8, 8, 8, 8, 8, 8, 8),)
+LOADS = ((4, 8, 16, 36),)
+CHUNKS = ((0, 64),)
 PINNED = True
 VECTOR_EVERY = 8
 HEAD_ON_SCALAR = 2
-MASK_SLOT = 10
 
 
 def tile_modelnew_t_kernel(tc, A, B, out):
@@ -82,23 +82,12 @@ def tile_modelnew_t_kernel(tc, A, B, out):
             for t0 in range(0, tiles, GROUP):
                 groups.append((ci, t0))
         n_groups = len(groups)
-        masked_group = [g for g in range(n_groups) if CHUNKS[groups[g][0]][0] == 0][0]
-        a_masked = const.tile([P, 4 * K], BF16)
-
         state = {}
         counter = [0]
 
-        def mask_a(t):
-            ci = groups[masked_group][0]
-            nc.vector.scalar_tensor_tensor(
-                out=a_masked[:, t * K : (t + 1) * K], in0=a_diff[:], scalar=float(t),
-                in1=a_tiles[ci][:, t * K : (t + 1) * K], op0=IS_LE, op1=MULT,
-            )
-
         def transposes(g):
             ci, t0 = groups[g]
-            src = a_masked if g == masked_group else a_tiles[ci]
-            words = src[:].bitcast(F32)
+            words = a_tiles[ci][:].bitcast(F32)
             banks = []
             for b in range(GROUP // 2):
                 xt = xt_pool.tile([P, 2, 2, P], F32, name="xt")
@@ -112,14 +101,22 @@ def tile_modelnew_t_kernel(tc, A, B, out):
             state[("xt", g)] = banks
 
         def regroup(g):
+            ci, t0 = groups[g]
             grp = work.tile([P, GROUP * P * 4], BF16, name="grp", align_bytes=64)
             view = grp[:].bitcast(F32).rearrange("p (r m u) -> p r m u", r=GROUP, u=2)
             for b, xt in enumerate(state[("xt", g)]):
+                if b == 1 and g >= 1:
+                    quantise(g - 1)
                 dst = view[:, 2 * b : 2 * b + 2, :, :]
                 if g < HEAD_ON_SCALAR:
                     nc.scalar.copy(out=dst, in_=xt[:].rearrange("p r u m -> p r m u"))
                 else:
                     nc.vector.tensor_copy(out=dst, in_=xt[:].rearrange("p r u m -> p r m u"))
+            corner = grp[:].rearrange("p (r m j) -> p r m j", r=GROUP, j=4)[:, :, 0:8, :]
+            nc.gpsimd.affine_select(
+                out=corner, in_=corner, pattern=[[1, GROUP], [64, 8], [-1, 4]],
+                compare_op=IS_GE, fill=0.0, base=t0, channel_multiplier=-4,
+            )
             state[("grp", g)] = grp
 
         def quantise(g):
@@ -179,13 +176,11 @@ def tile_modelnew_t_kernel(tc, A, B, out):
         for s in range(n_groups + 2):
             if s < n_groups:
                 transposes(s)
-            if 1 <= s <= n_groups:
+            if s == n_groups:
                 quantise(s - 1)
             if s >= 2:
                 multiply(s - 2)
             if s < n_groups:
                 regroup(s)
-            if MASK_SLOT <= s < MASK_SLOT + 4:
-                mask_a(s - MASK_SLOT)
             if s >= 2:
                 drain(s - 2)

@@ -13,7 +13,6 @@ U8 = mybir.dt.uint8
 FP8X4 = mybir.dt.float8_e4m3fn_x4
 MULT = mybir.AluOpType.mult
 IS_LE = mybir.AluOpType.is_le
-IS_GE = mybir.AluOpType.is_ge
 
 P = 128
 GROUP = 4
@@ -56,6 +55,11 @@ def tile_modelnew_t_kernel(tc, A, B, out):
             allow_small_or_imprecise_dtypes=True,
         )
 
+        c_diff = const.tile([P, GROUP, 8, 4], F32)
+        nc.gpsimd.iota(
+            c_diff[:], pattern=[[-1, GROUP], [-64, 8], [1, 4]], base=0, channel_multiplier=4,
+            allow_small_or_imprecise_dtypes=True,
+        )
         ident = const.tile([P, P], F32)
         make_identity(nc, ident[:])
         b_keep = const.tile([P, 4, N], BF16)
@@ -107,17 +111,23 @@ def tile_modelnew_t_kernel(tc, A, B, out):
             for b, xt in enumerate(state[("xt", g)]):
                 if b == 1 and g >= 1:
                     quantise(g - 1)
+                if b == 0 and g >= 1:
+                    mask(g - 1)
                 dst = view[:, 2 * b : 2 * b + 2, :, :]
                 if g < HEAD_ON_SCALAR:
                     nc.scalar.copy(out=dst, in_=xt[:].rearrange("p r u m -> p r m u"))
                 else:
                     nc.vector.tensor_copy(out=dst, in_=xt[:].rearrange("p r u m -> p r m u"))
             corner = grp[:].rearrange("p (r m j) -> p r m j", r=GROUP, j=4)[:, :, 0:8, :]
-            nc.gpsimd.affine_select(
-                out=corner, in_=corner, pattern=[[1, GROUP], [64, 8], [-1, 4]],
-                compare_op=IS_GE, fill=0.0, base=t0, channel_multiplier=-4,
-            )
+            state[("corner", g)] = corner
             state[("grp", g)] = grp
+
+        def mask(g):
+            ci, t0 = groups[g]
+            corner = state[("corner", g)]
+            nc.vector.scalar_tensor_tensor(
+                out=corner, in0=c_diff[:], scalar=float(t0), in1=corner, op0=IS_LE, op1=MULT
+            )
 
         def quantise(g):
             grp = state[("grp", g)]
@@ -177,6 +187,7 @@ def tile_modelnew_t_kernel(tc, A, B, out):
             if s < n_groups:
                 transposes(s)
             if s == n_groups:
+                mask(s - 1)
                 quantise(s - 1)
             if s >= 2:
                 multiply(s - 2)

@@ -38,7 +38,13 @@ def tile_modelnew_t_kernel(tc, A, B, out):
 
         a_tiles = []
         b_raw = const.tile([P, 4, N], BF16)
-        nc.sync.dma_start(out=b_raw[:], in_=B.rearrange("(p t) c -> p t c", t=4))
+        half = P // 2
+        b_rows = B.rearrange("(p t) c -> p t c", t=4)
+        nc.vector.memset(b_raw[0:half, :, N // 2 : N], 0.0)
+        nc.sync.dma_start(out=b_raw[half:P, :, :], in_=b_rows[half:P, :, :])
+        nc.scalar.dma_start(
+            out=b_raw[0:half, :, 0 : N // 2], in_=b_rows[0:half, :, 0 : N // 2]
+        )
         for ci, (row0, tiles) in enumerate(CHUNKS):
             a_sb = a_pool.tile([P, tiles * K], BF16, name="a%d" % ci)
             rows = A[row0 : row0 + P * tiles, :].rearrange("(p t) k -> p (t k)", t=tiles)

from contextlib import ExitStack

import concourse.mybir as mybir
from concourse.masks import make_identity

M, K, N = 8192, 512, 512
FLOPS = 2 * M * K * N

BF16 = mybir.dt.bfloat16
F32 = mybir.dt.float32
U32 = mybir.dt.uint32
U8 = mybir.dt.uint8
FP8X4 = mybir.dt.float8_e4m3fn_x4
MULT = mybir.AluOpType.mult
IS_LE = mybir.AluOpType.is_le

P = 128
GROUP = 4
STORES = ((8, 8, 8, 8, 8, 8, 8, 8),)
LOADS = ((4, 8, 16, 36),)
CHUNKS = ((0, 64),)
PINNED = True
VECTOR_EVERY = 8
HEAD_ON_SCALAR = 2


def tile_modelnew_t_kernel(tc, A, B, out):
    nc = tc.nc
    with ExitStack() as ctx:
        if PINNED:
            ctx.enter_context(tc.manual_schedule())
        const = ctx.enter_context(tc.tile_pool(name="const", bufs=1))
        a_pool = ctx.enter_context(tc.tile_pool(name="a", bufs=1))
        o_pool = ctx.enter_context(tc.tile_pool(name="o", bufs=1))
        work = ctx.enter_context(tc.tile_pool(name="work", bufs=3))
        xt_pool = ctx.enter_context(tc.psum_pool(name="xt", bufs=4))
        acc_pool = ctx.enter_context(tc.psum_pool(name="acc", bufs=4))

        a_tiles = []
        b_raw = const.tile([P, 4, N], BF16)
        half = P // 2
        b_rows = B.rearrange("(p t) c -> p t c", t=4)
        nc.vector.memset(b_raw[0:half, :, N // 2 : N], 0.0)
        nc.sync.dma_start(out=b_raw[half:P, :, :], in_=b_rows[half:P, :, :])
        nc.scalar.dma_start(
            out=b_raw[0:half, :, 0 : N // 2], in_=b_rows[0:half, :, 0 : N // 2]
        )
        for ci, (row0, tiles) in enumerate(CHUNKS):
            a_sb = a_pool.tile([P, tiles * K], BF16, name="a%d" % ci)
            rows = A[row0 : row0 + P * tiles, :].rearrange("(p t) k -> p (t k)", t=tiles)
            t0 = 0
            for width in LOADS[ci]:
                part = slice(t0 * K, (t0 + width) * K)
                nc.sync.dma_start(out=a_sb[:, part], in_=rows[:, part])
                t0 += width
            a_tiles.append(a_sb)

        a_diff = const.tile([P, K], F32)
        nc.gpsimd.iota(
            a_diff[:], pattern=[[1, K]], base=0, channel_multiplier=-4,
            allow_small_or_imprecise_dtypes=True,
        )

        c_diff = const.tile([P, GROUP, 8, 4], F32)
        nc.gpsimd.iota(
            c_diff[:], pattern=[[-1, GROUP], [-64, 8], [1, 4]], base=0, channel_multiplier=4,
            allow_small_or_imprecise_dtypes=True,
        )
        ident = const.tile([P, P], F32)
        make_identity(nc, ident[:])
        b_keep = const.tile([P, 4, N], BF16)
        for t in range(4):
            nc.vector.tensor_scalar(
                out=b_keep[:, t, :], in0=a_diff[:], scalar1=float(t), scalar2=None, op0=IS_LE
            )

        b_grp = const.tile([P, N * 4], BF16, align_bytes=64)
        b_codes = const.tile([P, N], U32, align_bytes=64)
        b_scl = const.tile([P, N], U8, align_bytes=64)

        def prepare_b():
            nc.vector.tensor_tensor(
                out=b_grp[:].rearrange("p (c t) -> p c t", t=4),
                in0=b_keep[:].rearrange("p t c -> p c t"),
                in1=b_raw[:].rearrange("p t c -> p c t"),
                op=MULT,
            )
            nc.vector.quantize_mx(out=b_codes[:].bitcast(FP8X4), scales=b_scl[:], in_=b_grp[:])

        groups = []
        for ci, (row0, tiles) in enumerate(CHUNKS):
            for t0 in range(0, tiles, GROUP):
                groups.append((ci, t0))
        n_groups = len(groups)
        state = {}
        counter = [0]

        def transposes(g):
            ci, t0 = groups[g]
            words = a_tiles[ci][:].bitcast(F32)
            banks = []
            for b in range(GROUP // 2):
                xt = xt_pool.tile([P, 2, 2, P], F32, name="xt")
                for r in range(2):
                    for u in range(2):
                        col = (t0 + 2 * b + r) * (K // 2)
                        nc.tensor.transpose(
                            xt[:, r, u, :], words[:, col + u : col + K // 2 : 2], ident[:]
                        )
                banks.append(xt)
            state[("xt", g)] = banks

        def regroup(g):
            ci, t0 = groups[g]
            grp = work.tile([P, GROUP * P * 4], BF16, name="grp", align_bytes=64)
            view = grp[:].bitcast(F32).rearrange("p (r m u) -> p r m u", r=GROUP, u=2)
            for b, xt in enumerate(state[("xt", g)]):
                if b == 1 and g >= 1:
                    quantise(g - 1)
                if b == 0 and g >= 1:
                    mask(g - 1)
                dst = view[:, 2 * b : 2 * b + 2, :, :]
                if g < HEAD_ON_SCALAR:
                    nc.scalar.copy(out=dst, in_=xt[:].rearrange("p r u m -> p r m u"))
                else:
                    nc.vector.tensor_copy(out=dst, in_=xt[:].rearrange("p r u m -> p r m u"))
            corner = grp[:].rearrange("p (r m j) -> p r m j", r=GROUP, j=4)[:, :, 0:8, :]
            state[("corner", g)] = corner
            state[("grp", g)] = grp

        def mask(g):
            ci, t0 = groups[g]
            corner = state[("corner", g)]
            nc.vector.scalar_tensor_tensor(
                out=corner, in0=c_diff[:], scalar=float(t0), in1=corner, op0=IS_LE, op1=MULT
            )

        def quantise(g):
            grp = state[("grp", g)]
            codes = work.tile([P, GROUP * P], U32, name="codes", align_bytes=64)
            scl = work.tile([P, GROUP * P], U8, name="scl", align_bytes=64)
            nc.vector.quantize_mx(out=codes[:].bitcast(FP8X4), scales=scl[:], in_=grp[:])
            state[("q", g)] = (codes, scl)

        def multiply(g):
            codes, scl = state[("q", g)]
            accs = []
            for r in range(GROUP):
                acc = acc_pool.tile([P, N], F32, name="acc")
                nc.tensor.matmul_mx(
                    out=acc[:],
                    lhsT=codes[:, r * P : (r + 1) * P].bitcast(FP8X4),
                    lhsT_scale=scl[:, r * P : (r + 1) * P],
                    rhs=b_codes[:].bitcast(FP8X4),
                    rhs_scale=b_scl[:],
                    start=True,
                    stop=True,
                )
                accs.append(acc)
            state[("acc", g)] = accs

        def drain(g):
            ci, t0 = groups[g]
            row0, tiles = CHUNKS[ci]
            first = 0
            unit = STORES[ci][0]
            for width in STORES[ci]:
                if first + width <= t0:
                    first += width
                else:
                    unit = width
                    break
            if t0 == first:
                state["o"] = o_pool.tile([P, unit, N], F32, name="o%d_%d" % (ci, first))
            o_sb = state["o"]
            for r, acc in enumerate(state[("acc", g)]):
                dst = o_sb[:, t0 + r - first, :]
                counter[0] += 1
                if counter[0] % VECTOR_EVERY == 0:
                    nc.vector.tensor_copy(out=dst, in_=acc[:])
                else:
                    nc.scalar.copy(out=dst, in_=acc[:])
            if t0 + GROUP == first + unit:
                nc.sync.dma_start(
                    out=out[row0 : row0 + P * tiles, :].rearrange("(p t) n -> p t n", t=tiles)[
                        :, first : first + unit, :
                    ],
                    in_=o_sb[:],
                )

        prepare_b()
        for s in range(n_groups + 2):
            if s < n_groups:
                transposes(s)
            if s == n_groups:
                mask(s - 1)
                quantise(s - 1)
            if s >= 2:
                multiply(s - 2)
            if s < n_groups:
                regroup(s)
            if s >= 2:
                drain(s - 2)
